import numpy as np
import ml_dtypes


def mxq(x, axis, fmt="e4m3"):
    dtype, down = {"e4m3": (ml_dtypes.float8_e4m3fn, 7), "e5m2": (ml_dtypes.float8_e5m2, 14)}[fmt]
    v = np.moveaxis(np.asarray(x, np.float32).astype(ml_dtypes.bfloat16).astype(np.float64), axis, -1)
    blocks = v.reshape(v.shape[:-1] + (-1, 32))
    amax = np.abs(blocks).max(-1, keepdims=True)
    byte = np.maximum(np.where(amax > 0, np.frexp(amax)[1] - 1 + 127, 0) - down, 1)
    scale = np.exp2(byte - 127.0)
    codes = (blocks / scale).astype(np.float32).astype(dtype).astype(np.float64)
    return np.moveaxis((codes * scale).reshape(v.shape), -1, axis)


WIDE = False


def mx_kscale(k):
    if not WIDE:
        return np.ones(k)
    levels = np.array([10, -10, 5, -5, 0])
    if k % 512:
        return np.exp2(np.random.permutation(np.resize(levels, k // 32))).repeat(32)
    a = np.empty((k // 512, 16))
    for p in range(k // 512):
        a[p, :8] = np.random.permutation(np.resize(levels, 8))
        for g in range(8):
            far = levels[np.abs(levels - a[p, g]) >= 10]
            a[p, g + 8] = far[np.random.randint(len(far))]
    return np.exp2(a.ravel()).repeat(32)


BF16 = ml_dtypes.bfloat16


def bf(x):
    return np.asarray(x, np.float32).astype(BF16)


def f64(x):
    return np.asarray(x).astype(np.float64)


H, A, NS, NE, M = 1024, 1024, 1024, 512, 1024


def setup_inputs():
    s, t = mx_kscale(H), mx_kscale(H)
    wsc = 0.25 / np.sqrt(H)
    return {
        "attendee_stmts": bf(np.random.standard_normal((NS, H)) * s),
        "attendee_eres": bf(np.random.standard_normal((NE, H)) * s),
        "attender": bf(np.random.standard_normal((M, H)) * 0.2 / t),
        "W_ss": bf(np.random.standard_normal((H, H)) * wsc * t[:, None] / s),
        "b_ss": bf(np.random.standard_normal(H) * 0.1 * t),
        "W_es": bf(np.random.standard_normal((H, H)) * wsc * t[:, None] / s),
        "b_es": bf(np.random.standard_normal(H) * 0.1 * t),
    }


def reference(attendee_stmts, attendee_eres, attender, W_ss, b_ss, W_es, b_es):
    aq = mxq(f64(attender), 1, "e4m3")
    p_ss = (mxq(f64(attendee_stmts), 1, "e4m3") @ mxq(f64(W_ss), 1, "e4m3").T) + f64(b_ss)
    p_es = (mxq(f64(attendee_eres), 1, "e4m3") @ mxq(f64(W_es), 1, "e4m3").T) + f64(b_es)
    scores_ss = mxq(p_ss, 1, "e4m3") @ aq.T
    scores_es = mxq(p_es, 1, "e4m3") @ aq.T
    return scores_ss, scores_es

@@ -1,0 +1,195 @@
+from contextlib import ExitStack
+
+import concourse.mybir as mybir
+from concourse.masks import make_identity
+
+F32 = mybir.dt.float32
+BF16 = mybir.dt.bfloat16
+U32 = mybir.dt.uint32
+U8 = mybir.dt.uint8
+FP8X4 = mybir.dt.float8_e4m3fn_x4
+
+P = 128
+H = 1024
+PACK = 4
+PASSES = H // (P * PACK)
+UNITS = 4
+SLAB = UNITS * P
+BANK = 512
+WORDS = H // 2
+M = 1024
+
+FLOPS = 2 * 2 * (1024 + 512) * H * H
+
+
+def unit_cols(j):
+    return slice(j * P, (j + 1) * P)
+
+
+def tile_attention_pa_kernel(
+    tc, attendee_stmts, attendee_eres, attender, W_ss, b_ss, W_es, b_es, out_0, out_1
+):
+    nc = tc.nc
+    with ExitStack() as ctx:
+        consts = ctx.enter_context(tc.tile_pool(name="consts", bufs=1))
+        raws = ctx.enter_context(tc.tile_pool(name="raws", bufs=1))
+        keep = ctx.enter_context(tc.tile_pool(name="keep", bufs=1))
+        stage = ctx.enter_context(tc.tile_pool(name="stage", bufs=6))
+        outs = ctx.enter_context(tc.tile_pool(name="outs", bufs=8))
+        psum = ctx.enter_context(tc.psum_pool(name="psum", bufs=8))
+        ctx.enter_context(tc.manual_schedule())
+
+        def load_slab(name, units):
+            raw = raws.tile([P, UNITS * H], BF16, name=name)
+            for j in range(UNITS):
+                nc.sync.dma_start(out=raw[:, j * H : (j + 1) * H], in_=units[j])
+            return raw
+
+        def plain_units(matrix, slab):
+            view = matrix.rearrange("(c j r) h -> c j r h", j=UNITS, r=P)
+            return [view[slab, j] for j in range(UNITS)]
+
+        def strided_units(weight, slab):
+            view = weight.rearrange("(c r t) h -> c t r h", r=P, t=PACK)
+            return [view[slab, t] for t in range(UNITS)]
+
+        raw_w_es = [load_slab("raw_w_es0", strided_units(W_es, 0))]
+        raw_x_es = load_slab("raw_x_es", plain_units(attendee_eres, 0))
+        raw_w_es.append(load_slab("raw_w_es1", strided_units(W_es, 1)))
+        raw_a = [load_slab("raw_a%d" % c, plain_units(attender, c)) for c in range(2)]
+        raw_w_ss = [load_slab("raw_w_ss0", strided_units(W_ss, 0))]
+        raw_x_ss = [load_slab("raw_x_ss0", plain_units(attendee_stmts, 0))]
+        raw_w_ss.append(load_slab("raw_w_ss1", strided_units(W_ss, 1)))
+        raw_x_ss.append(load_slab("raw_x_ss1", plain_units(attendee_stmts, 1)))
+
+        ident = consts.tile([P, P], F32, name="ident")
+        make_identity(nc, ident[:])
+
+        bias_rows = consts.tile([P, PACK * P], BF16, name="bias_rows")
+        nc.vector.memset(bias_rows[:], 0.0)
+        nc.scalar.dma_start(out=bias_rows[0:2, :], in_=b_ss.rearrange("(c w) -> c w", w=PACK * P))
+        nc.scalar.dma_start(out=bias_rows[2:4, :], in_=b_es.rearrange("(c w) -> c w", w=PACK * P))
+
+        def new_bank():
+            bank = psum.tile([P, BANK], F32, name="bank", tag="bank")
+            return bank
+
+        def spread_biases():
+            bank = new_bank()
+            words = bias_rows[:].bitcast(F32)
+            for u in range(2):
+                nc.tensor.transpose(bank[:, unit_cols(u)], words[:, u::2], ident[:])
+            bias_pairs = consts.tile([P, 16], BF16, name="bias_pairs")
+            nc.vector.tensor_copy(
+                out=bias_pairs[:].bitcast(F32).rearrange("p (s u) -> p s u", u=2),
+                in_=bank[:, 0 : 2 * P].rearrange("p (u s) -> p s u", u=2)[:, 0:4, :],
+            )
+            bias = consts.tile([P, 16], F32, name="bias")
+            nc.vector.tensor_copy(out=bias[:], in_=bias_pairs[:])
+            return bias
+
+        def new_operand(name):
+            codes = keep.tile([P, PASSES, SLAB], U32, name="%s_codes" % name, align_bytes=64)
+            scales = keep.tile([P, PASSES, SLAB], U8, name="%s_scales" % name, align_bytes=64)
+            return codes, scales
+
+        def quantise(grouped, operand, g, cols):
+            codes, scales = operand
+            nc.vector.quantize_mx(
+                out=codes[:, g, cols].bitcast(FP8X4), scales=scales[:, g, cols], in_=grouped
+            )
+
+        def transpose_slab(raw, name):
+            operand = new_operand(name)
+            raw_words = raw[:].bitcast(F32)
+            for j in range(UNITS):
+                bank = new_bank()
+                for c in range(WORDS // P):
+                    first_word = j * WORDS + (c // 2) * 2 * P + c % 2
+                    nc.tensor.transpose(
+                        bank[:, unit_cols(c)],
+                        raw_words[:, first_word : first_word + 2 * P - 1 : 2],
+                        ident[:],
+                    )
+                grouped = stage.tile([P, PASSES * P * PACK], BF16, name="grouped", align_bytes=64)
+                nc.scalar.copy(
+                    out=grouped[:].bitcast(F32).rearrange("p (g r u) -> p g r u", g=PASSES, u=2),
+                    in_=bank[:].rearrange("p (g u r) -> p g r u", g=PASSES, u=2),
+                )
+                for g in range(PASSES):
+                    quantise(grouped[:, g * P * PACK : (g + 1) * P * PACK], operand, g, unit_cols(j))
+            return operand
+
+        def mx_group(out, stationary, stationary_cols, moving, moving_cols):
+            for g in range(PASSES):
+                nc.tensor.matmul_mx(
+                    out=out,
+                    lhsT=stationary[0][:, g, stationary_cols].bitcast(FP8X4),
+                    lhsT_scale=stationary[1][:, g, stationary_cols],
+                    rhs=moving[0][:, g, moving_cols].bitcast(FP8X4),
+                    rhs_scale=moving[1][:, g, moving_cols],
+                    start=(g == 0),
+                    stop=(g == PASSES - 1),
+                )
+
+        def stage1(x, w, bias_cols, p, g2, units):
+            waiting = None
+            for j in units:
+                bank = new_bank()
+                for t in range(PACK):
+                    mx_group(bank[:, unit_cols(t)], w, unit_cols(t), x, unit_cols(j))
+                p_grouped = stage.tile([P, P, PACK], BF16, name="p_grouped", align_bytes=64)
+                nc.vector.tensor_tensor(
+                    out=p_grouped[:],
+                    in0=bank[:].rearrange("p (t s) -> p s t", t=PACK),
+                    in1=bias_cols.unsqueeze(1).to_broadcast([P, P, PACK]),
+                    op=mybir.AluOpType.add,
+                )
+                if waiting is not None:
+                    quantise(waiting[0], p, g2, unit_cols(waiting[1]))
+                waiting = (p_grouped[:].rearrange("p s t -> p (s t)"), j)
+            quantise(waiting[0], p, g2, unit_cols(waiting[1]))
+
+        def stage2(p, a, out_units, units, vector_helps):
+            for j in units:
+                scores = outs.tile([P, M], F32, name="scores")
+                for c in range(M // BANK):
+                    bank = new_bank()
+                    mx_group(bank[:], p, unit_cols(j), a[c], slice(0, SLAB))
+                    if vector_helps and c == 1:
+                        nc.vector.tensor_copy(out=scores[:, c * BANK : (c + 1) * BANK], in_=bank[:])
+                    else:
+                        nc.scalar.copy(out=scores[:, c * BANK : (c + 1) * BANK], in_=bank[:])
+                nc.sync.dma_start(out=out_units[j], in_=scores[:])
+
+        out_es = out_1.rearrange("(c j r) m -> c j r m", j=UNITS, r=P)
+        out_ss = out_0.rearrange("(c j r) m -> c j r m", j=UNITS, r=P)
+        p_es = new_operand("p_es")
+        p_ss = [new_operand("p_ss%d" % c) for c in range(2)]
+
+        first, second, whole = [0, 1], [2, 3], [0, 1, 2, 3]
+        w_es = [transpose_slab(raw_w_es[0], "w_es0")]
+        bias = spread_biases()
+        bias_ss = [bias[:, 4 * g2 : 4 * g2 + 4] for g2 in range(PASSES)]
+        bias_es = [bias[:, 8 + 4 * g2 : 8 + 4 * g2 + 4] for g2 in range(PASSES)]
+        x_es = transpose_slab(raw_x_es, "x_es")
+        stage1(x_es, w_es[0], bias_es[0], p_es, 0, first)
+        w_es.append(transpose_slab(raw_w_es[1], "w_es1"))
+        stage1(x_es, w_es[0], bias_es[0], p_es, 0, second)
+        a = [transpose_slab(raw_a[0], "a0")]
+        stage1(x_es, w_es[1], bias_es[1], p_es, 1, first)
+        a.append(transpose_slab(raw_a[1], "a1"))
+        stage1(x_es, w_es[1], bias_es[1], p_es, 1, second)
+        w_ss = [transpose_slab(raw_w_ss[0], "w_ss0")]
+        stage2(p_es, a, out_es[0], first, True)
+        x_ss = [transpose_slab(raw_x_ss[0], "x_ss0")]
+        stage2(p_es, a, out_es[0], second, True)
+        w_ss.append(transpose_slab(raw_w_ss[1], "w_ss1"))
+        stage1(x_ss[0], w_ss[0], bias_ss[0], p_ss[0], 0, whole)
+        x_ss.append(transpose_slab(raw_x_ss[1], "x_ss1"))
+        stage1(x_ss[0], w_ss[1], bias_ss[1], p_ss[0], 1, whole)
+        stage1(x_ss[1], w_ss[0], bias_ss[0], p_ss[1], 0, whole)
+        stage2(p_ss[0], a, out_ss[0], first, False)
+        stage1(x_ss[1], w_ss[1], bias_ss[1], p_ss[1], 1, whole)
+        stage2(p_ss[0], a, out_ss[0], second, False)
+        stage2(p_ss[1], a, out_ss[1], whole, False)

@@ -35,15 +35,18 @@ def tile_attention_pa_kernel(
         raws = ctx.enter_context(tc.tile_pool(name="raws", bufs=1))
         keep = ctx.enter_context(tc.tile_pool(name="keep", bufs=1))
         stage = ctx.enter_context(tc.tile_pool(name="stage", bufs=6))
+        sorts = ctx.enter_context(tc.tile_pool(name="sorts", bufs=12))
         outs = ctx.enter_context(tc.tile_pool(name="outs", bufs=8))
         psum = ctx.enter_context(tc.psum_pool(name="psum", bufs=8))
         ctx.enter_context(tc.manual_schedule())
 
-        def load_slab(name, units):
-            raw = raws.tile([P, UNITS * H], BF16, name=name)
-            for j in range(UNITS):
-                nc.sync.dma_start(out=raw[:, j * H : (j + 1) * H], in_=units[j])
-            return raw
+        def load_units(name, units):
+            tiles = []
+            for j, unit in enumerate(units):
+                raw = raws.tile([P, H], BF16, name="%s_%d" % (name, j))
+                nc.sync.dma_start(out=raw[:], in_=unit)
+                tiles.append(raw)
+            return tiles
 
         def plain_units(matrix, slab):
             view = matrix.rearrange("(c j r) h -> c j r h", j=UNITS, r=P)
@@ -53,14 +56,20 @@ def tile_attention_pa_kernel(
             view = weight.rearrange("(c r t) h -> c t r h", r=P, t=PACK)
             return [view[slab, t] for t in range(UNITS)]
 
-        raw_w_es = [load_slab("raw_w_es0", strided_units(W_es, 0))]
-        raw_x_es = load_slab("raw_x_es", plain_units(attendee_eres, 0))
-        raw_w_es.append(load_slab("raw_w_es1", strided_units(W_es, 1)))
-        raw_a = [load_slab("raw_a%d" % c, plain_units(attender, c)) for c in range(2)]
-        raw_w_ss = [load_slab("raw_w_ss0", strided_units(W_ss, 0))]
-        raw_x_ss = [load_slab("raw_x_ss0", plain_units(attendee_stmts, 0))]
-        raw_w_ss.append(load_slab("raw_w_ss1", strided_units(W_ss, 1)))
-        raw_x_ss.append(load_slab("raw_x_ss1", plain_units(attendee_stmts, 1)))
+        raw = {}
+        for name, units in (
+            ("w_es0", strided_units(W_es, 0)),
+            ("x_es", plain_units(attendee_eres, 0)),
+            ("w_es1", strided_units(W_es, 1)),
+            ("a0", plain_units(attender, 0)),
+            ("a1", plain_units(attender, 1)),
+            ("w_ss0", strided_units(W_ss, 0)),
+            ("x_ss0", plain_units(attendee_stmts, 0)),
+            ("w_ss1", strided_units(W_ss, 1)),
+            ("x_ss1", plain_units(attendee_stmts, 1)),
+        ):
+            raw[name] = load_units(name, units)
+        in_words = {}
 
         ident = consts.tile([P, P], F32, name="ident")
         make_identity(nc, ident[:])
@@ -88,6 +97,21 @@ def tile_attention_pa_kernel(
             nc.vector.tensor_copy(out=bias[:], in_=bias_pairs[:])
             return bias
 
+        def sort_unit(name, j, eng):
+            tile = raw[name][j]
+            words = sorts.tile([P, 2, WORDS // 2], F32, name="words")
+            src = tile[:].bitcast(F32).rearrange("p (n u) -> p u n", u=2)
+            if eng == "V": nc.vector.tensor_copy(out=words[:], in_=src)
+            elif eng == "S": nc.scalar.copy(out=words[:], in_=src)
+            else: nc.gpsimd.tensor_copy(out=words[:], in_=src)
+            in_words[name, j] = words
+
+        pending = []
+
+        def settle(left):
+            while len(pending) > left:
+                pending.pop(0)()
+
         def new_operand(name):
             codes = keep.tile([P, PASSES, SLAB], U32, name="%s_codes" % name, align_bytes=64)
             scales = keep.tile([P, PASSES, SLAB], U8, name="%s_scales" % name, align_bytes=64)
@@ -99,26 +123,36 @@ def tile_attention_pa_kernel(
                 out=codes[:, g, cols].bitcast(FP8X4), scales=scales[:, g, cols], in_=grouped
             )
 
-        def transpose_slab(raw, name):
-            operand = new_operand(name)
-            raw_words = raw[:].bitcast(F32)
-            for j in range(UNITS):
-                bank = new_bank()
-                for c in range(WORDS // P):
-                    first_word = j * WORDS + (c // 2) * 2 * P + c % 2
-                    nc.tensor.transpose(
-                        bank[:, unit_cols(c)],
-                        raw_words[:, first_word : first_word + 2 * P - 1 : 2],
-                        ident[:],
-                    )
-                grouped = stage.tile([P, PASSES * P * PACK], BF16, name="grouped", align_bytes=64)
-                nc.scalar.copy(
-                    out=grouped[:].bitcast(F32).rearrange("p (g r u) -> p g r u", g=PASSES, u=2),
-                    in_=bank[:].rearrange("p (g u r) -> p g r u", g=PASSES, u=2),
-                )
+        def transpose_unit(key, operand, j, ev):
+            tile = raw[key[0]][key[1]]
+            bank = new_bank()
+            words = in_words.get(key)
+            for g in range(PASSES):
+                for u in range(2):
+                    if words is None:
+                        first_word = g * 2 * P + u
+                        source = tile[:].bitcast(F32)[:, first_word : first_word + 2 * P - 1 : 2]
+                    else:
+                        source = words[:, u, unit_cols(g)]
+                    nc.tensor.transpose(bank[:, unit_cols(2 * g + u)], source, ident[:])
+            grouped = stage.tile([P, PASSES * P * PACK], BF16, name="grouped", align_bytes=64)
+            (nc.vector.tensor_copy if str(j) in ev else nc.scalar.copy)(
+                out=grouped[:].bitcast(F32).rearrange("p (g r u) -> p g r u", g=PASSES, u=2),
+                in_=bank[:].rearrange("p (g u r) -> p g r u", g=PASSES, u=2),
+            )
+
+            def finish():
                 for g in range(PASSES):
                     quantise(grouped[:, g * P * PACK : (g + 1) * P * PACK], operand, g, unit_cols(j))
-            return operand
+
+            pending.append(finish)
+
+        def transpose_slab(name, units, ev=""):
+            operand = operands.get(name) or new_operand(name)
+            operands[name] = operand
+            for j in units:
+                transpose_unit((name, j), operand, j, ev)
+                settle(1)
 
         def mx_group(out, stationary, stationary_cols, moving, moving_cols):
             for g in range(PASSES):
@@ -133,7 +167,7 @@ def tile_attention_pa_kernel(
                 )
 
         def stage1(x, w, bias_cols, p, g2, units):
-            waiting = None
+            x, w = operands[x], operands[w]
             for j in units:
                 bank = new_bank()
                 for t in range(PACK):
@@ -145,51 +179,71 @@ def tile_attention_pa_kernel(
                     in1=bias_cols.unsqueeze(1).to_broadcast([P, P, PACK]),
                     op=mybir.AluOpType.add,
                 )
-                if waiting is not None:
-                    quantise(waiting[0], p, g2, unit_cols(waiting[1]))
-                waiting = (p_grouped[:].rearrange("p s t -> p (s t)"), j)
-            quantise(waiting[0], p, g2, unit_cols(waiting[1]))
+                pending.append(
+                    lambda tile=p_grouped, j=j: quantise(tile[:].rearrange("p s t -> p (s t)"), p, g2, unit_cols(j))
+                )
+                settle(1)
 
-        def stage2(p, a, out_units, units, vector_helps):
+        def stage2(p, out_units, units, vector_banks):
             for j in units:
                 scores = outs.tile([P, M], F32, name="scores")
                 for c in range(M // BANK):
                     bank = new_bank()
-                    mx_group(bank[:], p, unit_cols(j), a[c], slice(0, SLAB))
-                    if vector_helps and c == 1:
-                        nc.vector.tensor_copy(out=scores[:, c * BANK : (c + 1) * BANK], in_=bank[:])
+                    mx_group(bank[:], p, unit_cols(j), operands["a%d" % c], slice(0, SLAB))
+                    part = slice(c * BANK, (c + 1) * BANK)
+                    if c in vector_banks:
+                        nc.vector.tensor_copy(out=scores[:, part], in_=bank[:])
                     else:
-                        nc.scalar.copy(out=scores[:, c * BANK : (c + 1) * BANK], in_=bank[:])
-                nc.sync.dma_start(out=out_units[j], in_=scores[:])
+                        nc.scalar.copy(out=scores[:, part], in_=bank[:])
+                    nc.sync.dma_start(out=out_units[j][:, part], in_=scores[:, part])
 
         out_es = out_1.rearrange("(c j r) m -> c j r m", j=UNITS, r=P)
         out_ss = out_0.rearrange("(c j r) m -> c j r m", j=UNITS, r=P)
+        operands = {}
         p_es = new_operand("p_es")
         p_ss = [new_operand("p_ss%d" % c) for c in range(2)]
 
-        first, second, whole = [0, 1], [2, 3], [0, 1, 2, 3]
-        w_es = [transpose_slab(raw_w_es[0], "w_es0")]
+        transpose_slab("w_es0", [0, 1, 2, 3])
         bias = spread_biases()
         bias_ss = [bias[:, 4 * g2 : 4 * g2 + 4] for g2 in range(PASSES)]
         bias_es = [bias[:, 8 + 4 * g2 : 8 + 4 * g2 + 4] for g2 in range(PASSES)]
-        x_es = transpose_slab(raw_x_es, "x_es")
-        stage1(x_es, w_es[0], bias_es[0], p_es, 0, first)
-        w_es.append(transpose_slab(raw_w_es[1], "w_es1"))
-        stage1(x_es, w_es[0], bias_es[0], p_es, 0, second)
-        a = [transpose_slab(raw_a[0], "a0")]
-        stage1(x_es, w_es[1], bias_es[1], p_es, 1, first)
-        a.append(transpose_slab(raw_a[1], "a1"))
-        stage1(x_es, w_es[1], bias_es[1], p_es, 1, second)
-        w_ss = [transpose_slab(raw_w_ss[0], "w_ss0")]
-        stage2(p_es, a, out_es[0], first, True)
-        x_ss = [transpose_slab(raw_x_ss[0], "x_ss0")]
-        stage2(p_es, a, out_es[0], second, True)
-        w_ss.append(transpose_slab(raw_w_ss[1], "w_ss1"))
-        stage1(x_ss[0], w_ss[0], bias_ss[0], p_ss[0], 0, whole)
-        x_ss.append(transpose_slab(raw_x_ss[1], "x_ss1"))
-        stage1(x_ss[0], w_ss[1], bias_ss[1], p_ss[0], 1, whole)
-        stage1(x_ss[1], w_ss[0], bias_ss[0], p_ss[1], 0, whole)
-        stage2(p_ss[0], a, out_ss[0], first, False)
-        stage1(x_ss[1], w_ss[1], bias_ss[1], p_ss[1], 1, whole)
-        stage2(p_ss[0], a, out_ss[0], second, False)
-        stage2(p_ss[1], a, out_ss[1], whole, False)
+        transpose_slab("x_es", [0, 1, 2, 3])
+        stage1("x_es", "w_es0", bias_es[0], p_es, 0, [0, 1])
+        transpose_slab("w_es1", [0, 1, 2, 3])
+        stage1("x_es", "w_es0", bias_es[0], p_es, 0, [2, 3])
+        transpose_slab("a0", [0, 1, 2, 3])
+        stage1("x_es", "w_es1", bias_es[1], p_es, 1, [0, 1])
+        transpose_slab("a1", [0, 1, 2, 3])
+        sort_unit("w_ss0", 0, "S")
+        sort_unit("w_ss0", 1, "S")
+        stage1("x_es", "w_es1", bias_es[1], p_es, 1, [2, 3])
+        transpose_slab("w_ss0", [0, 1, 2, 3])
+        settle(0)
+        sort_unit("x_ss0", 0, "S")
+        sort_unit("x_ss0", 1, "S")
+        sort_unit("x_ss0", 2, "V")
+        sort_unit("x_ss0", 3, "V")
+        stage2(p_es, out_es[0], [0, 1], [1])
+        transpose_slab("x_ss0", [0, 1, 2, 3])
+        sort_unit("w_ss1", 0, "S")
+        sort_unit("w_ss1", 1, "S")
+        sort_unit("w_ss1", 2, "V")
+        sort_unit("w_ss1", 3, "V")
+        stage2(p_es, out_es[0], [2, 3], [1])
+        transpose_slab("w_ss1", [0, 1, 2, 3])
+        settle(0)
+        sort_unit("x_ss1", 0, "S")
+        sort_unit("x_ss1", 1, "S")
+        sort_unit("x_ss1", 2, "S")
+        sort_unit("x_ss1", 3, "S")
+        stage1("x_ss0", "w_ss0", bias_ss[0], p_ss[0], 0, [0, 1, 2, 3])
+        settle(0)
+        stage1("x_ss0", "w_ss1", bias_ss[1], p_ss[0], 1, [0, 1, 2, 3])
+        transpose_slab("x_ss1", [0, 1, 2, 3])
+        settle(0)
+        stage2(p_ss[0], out_ss[0], [0, 1], [1])
+        stage1("x_ss1", "w_ss0", bias_ss[0], p_ss[1], 0, [0, 1, 2, 3])
+        stage2(p_ss[0], out_ss[0], [2, 3], [])
+        stage1("x_ss1", "w_ss1", bias_ss[1], p_ss[1], 1, [0, 1, 2, 3])
+        settle(0)
+        stage2(p_ss[1], out_ss[1], [0, 1, 2, 3], [1])

@@ -57,17 +57,19 @@ def tile_attention_pa_kernel(
             return [view[slab, t] for t in range(UNITS)]
 
         raw = {}
-        for name, units in (
-            ("w_es0", strided_units(W_es, 0)),
-            ("x_es", plain_units(attendee_eres, 0)),
-            ("w_es1", strided_units(W_es, 1)),
-            ("a0", plain_units(attender, 0)),
-            ("a1", plain_units(attender, 1)),
-            ("w_ss0", strided_units(W_ss, 0)),
-            ("x_ss0", plain_units(attendee_stmts, 0)),
-            ("w_ss1", strided_units(W_ss, 1)),
-            ("x_ss1", plain_units(attendee_stmts, 1)),
-        ):
+        sources = {
+            "w_es0": strided_units(W_es, 0),
+            "x_es": plain_units(attendee_eres, 0),
+            "w_es1": strided_units(W_es, 1),
+            "a0": plain_units(attender, 0),
+            "a1": plain_units(attender, 1),
+            "w_ss0": strided_units(W_ss, 0),
+            "x_ss0": plain_units(attendee_stmts, 0),
+            "w_ss1": strided_units(W_ss, 1),
+            "x_ss1": plain_units(attendee_stmts, 1),
+        }
+        for name in ["w_ss0","x_ss0","w_ss1","a0","a1","x_ss1","w_es0","x_es","w_es1"]:
+            units = sources[name]
             raw[name] = load_units(name, units)
         in_words = {}
 
@@ -112,18 +114,27 @@ def tile_attention_pa_kernel(
             while len(pending) > left:
                 pending.pop(0)()
 
-        def new_operand(name):
-            codes = keep.tile([P, PASSES, SLAB], U32, name="%s_codes" % name, align_bytes=64)
-            scales = keep.tile([P, PASSES, SLAB], U8, name="%s_scales" % name, align_bytes=64)
-            return codes, scales
+        def new_operand(name, by_unit):
+            shape = [P, UNITS, PASSES, P] if by_unit else [P, PASSES, SLAB]
+            codes = keep.tile(shape, U32, name="%s_codes" % name, align_bytes=64)
+            scales = keep.tile(shape, U8, name="%s_scales" % name, align_bytes=64)
+            return codes, scales, by_unit
 
-        def quantise(grouped, operand, g, cols):
-            codes, scales = operand
-            nc.vector.quantize_mx(
-                out=codes[:, g, cols].bitcast(FP8X4), scales=scales[:, g, cols], in_=grouped
-            )
+        def unit_of(operand, g, j):
+            codes, scales, by_unit = operand
+            if by_unit:
+                return codes[:, j, g, :], scales[:, j, g, :]
+            return codes[:, g, unit_cols(j)], scales[:, g, unit_cols(j)]
 
-        def transpose_unit(key, operand, j, ev):
+        def slab_of(operand, g):
+            codes, scales, by_unit = operand
+            return codes[:, g, :], scales[:, g, :]
+
+        def quantise(grouped, target):
+            codes, scales = target
+            nc.vector.quantize_mx(out=codes.bitcast(FP8X4), scales=scales, in_=grouped)
+
+        def transpose_unit(key, grouped, half, ev):
             tile = raw[key[0]][key[1]]
             bank = new_bank()
             words = in_words.get(key)
@@ -135,115 +146,165 @@ def tile_attention_pa_kernel(
                     else:
                         source = words[:, u, unit_cols(g)]
                     nc.tensor.transpose(bank[:, unit_cols(2 * g + u)], source, ident[:])
-            grouped = stage.tile([P, PASSES * P * PACK], BF16, name="grouped", align_bytes=64)
-            (nc.vector.tensor_copy if str(j) in ev else nc.scalar.copy)(
-                out=grouped[:].bitcast(F32).rearrange("p (g r u) -> p g r u", g=PASSES, u=2),
+            (nc.vector.tensor_copy if str(key[1]) in ev else nc.scalar.copy)(
+                out=grouped[:].bitcast(F32).rearrange("p (g h r u) -> p g h r u", g=PASSES, r=P, u=2)[:, :, half],
                 in_=bank[:].rearrange("p (g u r) -> p g r u", g=PASSES, u=2),
             )
 
-            def finish():
-                for g in range(PASSES):
-                    quantise(grouped[:, g * P * PACK : (g + 1) * P * PACK], operand, g, unit_cols(j))
-
-            pending.append(finish)
-
         def transpose_slab(name, units, ev=""):
-            operand = operands.get(name) or new_operand(name)
+            operand = operands.get(name) or new_operand(name, name[0] != "a")
             operands[name] = operand
-            for j in units:
-                transpose_unit((name, j), operand, j, ev)
+            codes, scales, by_unit = operand
+            step = 1 if by_unit else 2
+            for j in units[::step]:
+                grouped = stage.tile([P, step * H], BF16, name="grouped%d" % step, align_bytes=64)
+                for half in range(step):
+                    transpose_unit((name, j + half), grouped, half, ev)
+                    if half + 1 < step:
+                        settle(0)
+
+                def finish(grouped=grouped, j=j):
+                    if by_unit:
+                        targets = [[part[:, j].rearrange("p g r -> p (g r)") for part in (codes, scales)]]
+                    else:
+                        cols = slice(j * P, (j + 2) * P)
+                        targets = [[part[:, g, cols] for part in (codes, scales)] for g in range(PASSES)]
+                    for i, target in enumerate(targets):
+                        width = step * H // len(targets)
+                        quantise(grouped[:, i * width : (i + 1) * width], target)
+
+                pending.append(finish)
                 settle(1)
 
-        def mx_group(out, stationary, stationary_cols, moving, moving_cols):
+        def mx_group(out, stationary, moving):
             for g in range(PASSES):
+                lhs, rhs = stationary(g), moving(g)
                 nc.tensor.matmul_mx(
                     out=out,
-                    lhsT=stationary[0][:, g, stationary_cols].bitcast(FP8X4),
-                    lhsT_scale=stationary[1][:, g, stationary_cols],
-                    rhs=moving[0][:, g, moving_cols].bitcast(FP8X4),
-                    rhs_scale=moving[1][:, g, moving_cols],
+                    lhsT=lhs[0].bitcast(FP8X4),
+                    lhsT_scale=lhs[1],
+                    rhs=rhs[0].bitcast(FP8X4),
+                    rhs_scale=rhs[1],
                     start=(g == 0),
                     stop=(g == PASSES - 1),
                 )
 
         def stage1(x, w, bias_cols, p, g2, units):
             x, w = operands[x], operands[w]
+            group = []
             for j in units:
                 bank = new_bank()
                 for t in range(PACK):
-                    mx_group(bank[:, unit_cols(t)], w, unit_cols(t), x, unit_cols(j))
-                p_grouped = stage.tile([P, P, PACK], BF16, name="p_grouped", align_bytes=64)
+                    mx_group(
+                        bank[:, unit_cols(t)],
+                        lambda g, t=t: unit_of(w, g, t),
+                        lambda g, j=j: unit_of(x, g, j),
+                    )
+                if len(group) == 0:
+                    p_grouped = stage.tile([P, 2 * P, PACK], BF16, name="p_grouped", align_bytes=64)
                 nc.vector.tensor_tensor(
-                    out=p_grouped[:],
+                    out=p_grouped[:, len(group) * P : (len(group) + 1) * P, :],
                     in0=bank[:].rearrange("p (t s) -> p s t", t=PACK),
                     in1=bias_cols.unsqueeze(1).to_broadcast([P, P, PACK]),
                     op=mybir.AluOpType.add,
                 )
-                pending.append(
-                    lambda tile=p_grouped, j=j: quantise(tile[:].rearrange("p s t -> p (s t)"), p, g2, unit_cols(j))
-                )
-                settle(1)
+                group.append(j)
+                settle(0)
+                if len(group) == 2 or j == units[-1]:
+                    cols = slice(group[0] * P, (group[-1] + 1) * P)
+                    used = len(group) * P
+                    group = []
+                    pending.append(
+                        lambda tile=p_grouped, cols=cols, used=used: quantise(
+                            tile[:, :used, :].rearrange("p s t -> p (s t)"), [part[:, g2, cols] for part in p[:2]]
+                        )
+                    )
+
+        def score_bank(p, out_unit, j, c, scores, vector_banks):
+            bank = new_bank()
+            mx_group(bank[:], lambda g: unit_of(p, g, j), lambda g: slab_of(operands["a%d" % c], g))
+            part = slice(c * BANK, (c + 1) * BANK)
+            if c in vector_banks:
+                nc.vector.tensor_copy(out=scores[:, part], in_=bank[:])
+            else:
+                nc.scalar.copy(out=scores[:, part], in_=bank[:])
+            if c == 1:
+                nc.sync.dma_start(out=out_unit, in_=scores[:])
 
         def stage2(p, out_units, units, vector_banks):
             for j in units:
                 scores = outs.tile([P, M], F32, name="scores")
                 for c in range(M // BANK):
-                    bank = new_bank()
-                    mx_group(bank[:], p, unit_cols(j), operands["a%d" % c], slice(0, SLAB))
-                    part = slice(c * BANK, (c + 1) * BANK)
-                    if c in vector_banks:
-                        nc.vector.tensor_copy(out=scores[:, part], in_=bank[:])
-                    else:
-                        nc.scalar.copy(out=scores[:, part], in_=bank[:])
-                    nc.sync.dma_start(out=out_units[j][:, part], in_=scores[:, part])
+                    score_bank(p, out_units[j], j, c, scores, vector_banks)
+
+        def last_scores(p, out_unit, j):
+            scores = outs.tile([P, M], F32, name="scores")
+            score_bank(p, out_unit, j, 0, scores, [])
+            nc.sync.dma_start(out=out_unit[:, :BANK], in_=scores[:, :BANK])
+            for half in range(2):
+                bank = new_bank()
+                cols = slice(half * BANK // 2, (half + 1) * BANK // 2)
+                mx_group(
+                    bank[:, : BANK // 2],
+                    lambda g: unit_of(p, g, j),
+                    lambda g: tuple(part[:, cols] for part in slab_of(operands["a1"], g)),
+                )
+                part = slice(BANK + half * BANK // 2, BANK + (half + 1) * BANK // 2)
+                copy = nc.scalar.copy if half else nc.vector.tensor_copy
+                copy(out=scores[:, part], in_=bank[:, : BANK // 2])
+                nc.sync.dma_start(out=out_unit[:, part], in_=scores[:, part])
 
         out_es = out_1.rearrange("(c j r) m -> c j r m", j=UNITS, r=P)
         out_ss = out_0.rearrange("(c j r) m -> c j r m", j=UNITS, r=P)
         operands = {}
-        p_es = new_operand("p_es")
-        p_ss = [new_operand("p_ss%d" % c) for c in range(2)]
+        p_es = new_operand("p_es", False)
+        p_ss = [new_operand("p_ss%d" % c, False) for c in range(2)]
 
-        transpose_slab("w_es0", [0, 1, 2, 3])
+        transpose_slab("w_ss0", [0, 1, 2, 3])
         bias = spread_biases()
         bias_ss = [bias[:, 4 * g2 : 4 * g2 + 4] for g2 in range(PASSES)]
         bias_es = [bias[:, 8 + 4 * g2 : 8 + 4 * g2 + 4] for g2 in range(PASSES)]
-        transpose_slab("x_es", [0, 1, 2, 3])
-        stage1("x_es", "w_es0", bias_es[0], p_es, 0, [0, 1])
-        transpose_slab("w_es1", [0, 1, 2, 3])
-        stage1("x_es", "w_es0", bias_es[0], p_es, 0, [2, 3])
-        transpose_slab("a0", [0, 1, 2, 3])
-        stage1("x_es", "w_es1", bias_es[1], p_es, 1, [0, 1])
-        transpose_slab("a1", [0, 1, 2, 3])
-        sort_unit("w_ss0", 0, "S")
-        sort_unit("w_ss0", 1, "S")
-        stage1("x_es", "w_es1", bias_es[1], p_es, 1, [2, 3])
-        transpose_slab("w_ss0", [0, 1, 2, 3])
-        settle(0)
-        sort_unit("x_ss0", 0, "S")
-        sort_unit("x_ss0", 1, "S")
-        sort_unit("x_ss0", 2, "V")
-        sort_unit("x_ss0", 3, "V")
-        stage2(p_es, out_es[0], [0, 1], [1])
         transpose_slab("x_ss0", [0, 1, 2, 3])
-        sort_unit("w_ss1", 0, "S")
-        sort_unit("w_ss1", 1, "S")
-        sort_unit("w_ss1", 2, "V")
-        sort_unit("w_ss1", 3, "V")
-        stage2(p_es, out_es[0], [2, 3], [1])
+        stage1("x_ss0", "w_ss0", bias_ss[0], p_ss[0], 0, [0, 1])
         transpose_slab("w_ss1", [0, 1, 2, 3])
-        settle(0)
-        sort_unit("x_ss1", 0, "S")
-        sort_unit("x_ss1", 1, "S")
+        sort_unit("a0", 2, "S")
+        sort_unit("a0", 3, "S")
+        stage1("x_ss0", "w_ss0", bias_ss[0], p_ss[0], 0, [2, 3])
+        transpose_slab("a0", [0, 1, 2, 3])
+        sort_unit("a1", 2, "S")
+        sort_unit("a1", 3, "S")
+        stage1("x_ss0", "w_ss1", bias_ss[1], p_ss[0], 1, [0, 1])
+        transpose_slab("a1", [0, 1, 2, 3])
         sort_unit("x_ss1", 2, "S")
         sort_unit("x_ss1", 3, "S")
-        stage1("x_ss0", "w_ss0", bias_ss[0], p_ss[0], 0, [0, 1, 2, 3])
-        settle(0)
-        stage1("x_ss0", "w_ss1", bias_ss[1], p_ss[0], 1, [0, 1, 2, 3])
+        stage1("x_ss0", "w_ss1", bias_ss[1], p_ss[0], 1, [2, 3])
         transpose_slab("x_ss1", [0, 1, 2, 3])
         settle(0)
-        stage2(p_ss[0], out_ss[0], [0, 1], [1])
-        stage1("x_ss1", "w_ss0", bias_ss[0], p_ss[1], 0, [0, 1, 2, 3])
+        sort_unit("w_es0", 0, "V")
+        sort_unit("w_es0", 1, "V")
+        sort_unit("w_es0", 2, "V")
+        sort_unit("w_es0", 3, "V")
+        stage2(p_ss[0], out_ss[0], [0, 1], [])
+        transpose_slab("w_es0", [0, 1, 2, 3])
+        sort_unit("x_es", 0, "V")
+        sort_unit("x_es", 1, "V")
+        sort_unit("x_es", 2, "V")
+        sort_unit("x_es", 3, "V")
         stage2(p_ss[0], out_ss[0], [2, 3], [])
+        stage1("x_ss1", "w_ss0", bias_ss[0], p_ss[1], 0, [0, 1])
+        transpose_slab("x_es", [0, 1, 2, 3])
+        stage1("x_ss1", "w_ss0", bias_ss[0], p_ss[1], 0, [2, 3])
+        sort_unit("w_es1", 0, "S")
+        sort_unit("w_es1", 1, "S")
+        sort_unit("w_es1", 2, "S")
+        sort_unit("w_es1", 3, "S")
         stage1("x_ss1", "w_ss1", bias_ss[1], p_ss[1], 1, [0, 1, 2, 3])
+        transpose_slab("w_es1", [0, 1, 2, 3])
+        stage2(p_ss[1], out_ss[1], [0, 1, 2], [])
         settle(0)
-        stage2(p_ss[1], out_ss[1], [0, 1, 2, 3], [1])
+        stage1("x_es", "w_es0", bias_es[0], p_es, 0, [0, 1, 2, 3])
+        stage2(p_ss[1], out_ss[1], [3], [])
+        stage1("x_es", "w_es1", bias_es[1], p_es, 1, [0, 1, 2, 3])
+        settle(0)
+        stage2(p_es, out_es[0], [0, 1, 2], [1])
+        last_scores(p_es, out_es[0][3], 3)

@@ -85,6 +85,16 @@ def tile_attention_pa_kernel(
             bank = psum.tile([P, BANK], F32, name="bank", tag="bank")
             return bank
 
+        warm = {}
+
+        def warm_up(passes):
+            if not warm:
+                warm["zeros"] = consts.tile([P, BANK], BF16, name="zeros")
+                nc.vector.memset(warm["zeros"][:], 0.0)
+            bank = new_bank()
+            for i in range(passes):
+                nc.tensor.matmul(bank[:], warm["zeros"][:, 0:P], warm["zeros"][:], start=True, stop=True)
+
         def spread_biases():
             bank = new_bank()
             words = bias_rows[:].bitcast(F32)
@@ -260,46 +270,69 @@ def tile_attention_pa_kernel(
         p_es = new_operand("p_es", False)
         p_ss = [new_operand("p_ss%d" % c, False) for c in range(2)]
 
-        transpose_slab("w_ss0", [0, 1, 2, 3])
+        warm_up(5)
+        transpose_slab("w_ss0", [0])
+        warm_up(1)
+        transpose_slab("w_ss0", [1, 2])
+        warm_up(1)
+        transpose_slab("w_ss0", [3])
         bias = spread_biases()
         bias_ss = [bias[:, 4 * g2 : 4 * g2 + 4] for g2 in range(PASSES)]
         bias_es = [bias[:, 8 + 4 * g2 : 8 + 4 * g2 + 4] for g2 in range(PASSES)]
-        transpose_slab("x_ss0", [0, 1, 2, 3])
+        transpose_slab("x_ss0", [0])
+        warm_up(1)
+        transpose_slab("x_ss0", [1, 2])
+        warm_up(1)
+        transpose_slab("x_ss0", [3])
         stage1("x_ss0", "w_ss0", bias_ss[0], p_ss[0], 0, [0, 1])
-        transpose_slab("w_ss1", [0, 1, 2, 3])
+        transpose_slab("w_ss1", [0, 1])
+        warm_up(1)
+        transpose_slab("w_ss1", [2, 3])
         sort_unit("a0", 2, "S")
         sort_unit("a0", 3, "S")
         stage1("x_ss0", "w_ss0", bias_ss[0], p_ss[0], 0, [2, 3])
-        transpose_slab("a0", [0, 1, 2, 3])
+        transpose_slab("a0", [0, 1])
+        warm_up(1)
+        transpose_slab("a0", [2, 3])
         sort_unit("a1", 2, "S")
         sort_unit("a1", 3, "S")
         stage1("x_ss0", "w_ss1", bias_ss[1], p_ss[0], 1, [0, 1])
-        transpose_slab("a1", [0, 1, 2, 3])
+        transpose_slab("a1", [0, 1])
+        warm_up(1)
+        transpose_slab("a1", [2, 3])
         sort_unit("x_ss1", 2, "S")
         sort_unit("x_ss1", 3, "S")
         stage1("x_ss0", "w_ss1", bias_ss[1], p_ss[0], 1, [2, 3])
-        transpose_slab("x_ss1", [0, 1, 2, 3])
+        transpose_slab("x_ss1", [0, 1])
+        warm_up(1)
+        transpose_slab("x_ss1", [2, 3])
         settle(0)
         sort_unit("w_es0", 0, "V")
         sort_unit("w_es0", 1, "V")
         sort_unit("w_es0", 2, "V")
         sort_unit("w_es0", 3, "V")
         stage2(p_ss[0], out_ss[0], [0, 1], [])
-        transpose_slab("w_es0", [0, 1, 2, 3])
+        transpose_slab("w_es0", [0, 1])
+        warm_up(1)
+        transpose_slab("w_es0", [2, 3])
         sort_unit("x_es", 0, "V")
         sort_unit("x_es", 1, "V")
         sort_unit("x_es", 2, "V")
         sort_unit("x_es", 3, "V")
         stage2(p_ss[0], out_ss[0], [2, 3], [])
         stage1("x_ss1", "w_ss0", bias_ss[0], p_ss[1], 0, [0, 1])
-        transpose_slab("x_es", [0, 1, 2, 3])
+        transpose_slab("x_es", [0, 1])
+        warm_up(1)
+        transpose_slab("x_es", [2, 3])
         stage1("x_ss1", "w_ss0", bias_ss[0], p_ss[1], 0, [2, 3])
         sort_unit("w_es1", 0, "S")
         sort_unit("w_es1", 1, "S")
         sort_unit("w_es1", 2, "S")
         sort_unit("w_es1", 3, "S")
         stage1("x_ss1", "w_ss1", bias_ss[1], p_ss[1], 1, [0, 1, 2, 3])
-        transpose_slab("w_es1", [0, 1, 2, 3])
+        transpose_slab("w_es1", [0, 1])
+        warm_up(1)
+        transpose_slab("w_es1", [2, 3])
         stage2(p_ss[1], out_ss[1], [0, 1, 2], [])
         settle(0)
         stage1("x_es", "w_es0", bias_es[0], p_es, 0, [0, 1, 2, 3])

@@ -271,73 +271,63 @@ def tile_attention_pa_kernel(
         p_ss = [new_operand("p_ss%d" % c, False) for c in range(2)]
 
         warm_up(5)
-        transpose_slab("w_ss0", [0])
+        transpose_slab("w_ss0", [0, 1, 2, 3])
         warm_up(1)
-        transpose_slab("w_ss0", [1, 2])
+        transpose_slab("x_ss0", [0, 1])
         warm_up(1)
-        transpose_slab("w_ss0", [3])
+        transpose_slab("x_ss0", [2])
+        warm_up(1)
         bias = spread_biases()
         bias_ss = [bias[:, 4 * g2 : 4 * g2 + 4] for g2 in range(PASSES)]
         bias_es = [bias[:, 8 + 4 * g2 : 8 + 4 * g2 + 4] for g2 in range(PASSES)]
-        transpose_slab("x_ss0", [0])
-        warm_up(1)
-        transpose_slab("x_ss0", [1, 2])
-        warm_up(1)
         transpose_slab("x_ss0", [3])
         stage1("x_ss0", "w_ss0", bias_ss[0], p_ss[0], 0, [0, 1])
-        transpose_slab("w_ss1", [0, 1])
-        warm_up(1)
-        transpose_slab("w_ss1", [2, 3])
+        transpose_slab("w_ss1", [0, 1, 2, 3])
         sort_unit("a0", 2, "S")
-        sort_unit("a0", 3, "S")
+        sort_unit("a0", 3, "V")
         stage1("x_ss0", "w_ss0", bias_ss[0], p_ss[0], 0, [2, 3])
-        transpose_slab("a0", [0, 1])
-        warm_up(1)
-        transpose_slab("a0", [2, 3])
+        transpose_slab("a0", [0, 1, 2, 3])
         sort_unit("a1", 2, "S")
-        sort_unit("a1", 3, "S")
+        sort_unit("a1", 3, "V")
         stage1("x_ss0", "w_ss1", bias_ss[1], p_ss[0], 1, [0, 1])
-        transpose_slab("a1", [0, 1])
-        warm_up(1)
-        transpose_slab("a1", [2, 3])
+        transpose_slab("a1", [0, 1, 2, 3])
         sort_unit("x_ss1", 2, "S")
-        sort_unit("x_ss1", 3, "S")
+        sort_unit("x_ss1", 3, "V")
         stage1("x_ss0", "w_ss1", bias_ss[1], p_ss[0], 1, [2, 3])
-        transpose_slab("x_ss1", [0, 1])
-        warm_up(1)
-        transpose_slab("x_ss1", [2, 3])
-        settle(0)
         sort_unit("w_es0", 0, "V")
         sort_unit("w_es0", 1, "V")
         sort_unit("w_es0", 2, "V")
         sort_unit("w_es0", 3, "V")
+        transpose_slab("x_ss1", [0, 1, 2, 3])
+        settle(0)
         stage2(p_ss[0], out_ss[0], [0, 1], [])
-        transpose_slab("w_es0", [0, 1])
-        warm_up(1)
-        transpose_slab("w_es0", [2, 3])
         sort_unit("x_es", 0, "V")
         sort_unit("x_es", 1, "V")
         sort_unit("x_es", 2, "V")
         sort_unit("x_es", 3, "V")
+        transpose_slab("w_es0", [0, 1, 2, 3])
         stage2(p_ss[0], out_ss[0], [2, 3], [])
         stage1("x_ss1", "w_ss0", bias_ss[0], p_ss[1], 0, [0, 1])
-        transpose_slab("x_es", [0, 1])
-        warm_up(1)
-        transpose_slab("x_es", [2, 3])
+        sort_unit("w_es1", 0, "V")
+        sort_unit("w_es1", 1, "V")
+        sort_unit("w_es1", 2, "V")
+        sort_unit("w_es1", 3, "V")
+        transpose_slab("x_es", [0, 1, 2, 3])
         stage1("x_ss1", "w_ss0", bias_ss[0], p_ss[1], 0, [2, 3])
-        sort_unit("w_es1", 0, "S")
-        sort_unit("w_es1", 1, "S")
-        sort_unit("w_es1", 2, "S")
-        sort_unit("w_es1", 3, "S")
-        stage1("x_ss1", "w_ss1", bias_ss[1], p_ss[1], 1, [0, 1, 2, 3])
-        transpose_slab("w_es1", [0, 1])
-        warm_up(1)
-        transpose_slab("w_es1", [2, 3])
-        stage2(p_ss[1], out_ss[1], [0, 1, 2], [])
+        stage1("x_ss1", "w_ss1", bias_ss[1], p_ss[1], 1, [0, 1])
+        transpose_slab("w_es1", [0, 1, 2, 3])
+        stage1("x_ss1", "w_ss1", bias_ss[1], p_ss[1], 1, [2, 3])
+        stage1("x_es", "w_es0", bias_es[0], p_es, 0, [0, 1])
+        stage2(p_ss[1], out_ss[1], [0], [])
+        stage1("x_es", "w_es0", bias_es[0], p_es, 0, [2, 3])
+        stage2(p_ss[1], out_ss[1], [1], [])
+        stage1("x_es", "w_es1", bias_es[1], p_es, 1, [0, 1])
+        stage2(p_ss[1], out_ss[1], [2], [])
+        stage1("x_es", "w_es1", bias_es[1], p_es, 1, [2])
+        stage2(p_ss[1], out_ss[1], [3], [1])
+        stage1("x_es", "w_es1", bias_es[1], p_es, 1, [3])
+        stage2(p_es, out_es[0], [0], [1])
+        stage2(p_es, out_es[0], [1], [1])
         settle(0)
-        stage1("x_es", "w_es0", bias_es[0], p_es, 0, [0, 1, 2, 3])
-        stage2(p_ss[1], out_ss[1], [3], [])
-        stage1("x_es", "w_es1", bias_es[1], p_es, 1, [0, 1, 2, 3])
-        settle(0)
-        stage2(p_es, out_es[0], [0, 1, 2], [1])
+        stage2(p_es, out_es[0], [2], [1])
         last_scores(p_es, out_es[0][3], 3)

@@ -77,6 +77,9 @@ def tile_attention_pa_kernel(
         make_identity(nc, ident[:])
 
         bias_rows = consts.tile([P, PACK * P], BF16, name="bias_rows")
+        zeros = consts.tile([P, BANK], BF16, name="zeros")
+        nc.vector.memset(zeros[:, 0:P], 0.0)
+        nc.vector.memset(zeros[:, P:], 0.0)
         nc.vector.memset(bias_rows[:], 0.0)
         nc.scalar.dma_start(out=bias_rows[0:2, :], in_=b_ss.rearrange("(c w) -> c w", w=PACK * P))
         nc.scalar.dma_start(out=bias_rows[2:4, :], in_=b_es.rearrange("(c w) -> c w", w=PACK * P))
@@ -85,15 +88,10 @@ def tile_attention_pa_kernel(
             bank = psum.tile([P, BANK], F32, name="bank", tag="bank")
             return bank
 
-        warm = {}
-
-        def warm_up(passes):
-            if not warm:
-                warm["zeros"] = consts.tile([P, BANK], BF16, name="zeros")
-                nc.vector.memset(warm["zeros"][:], 0.0)
+        def warm_up(passes, width):
             bank = new_bank()
             for i in range(passes):
-                nc.tensor.matmul(bank[:], warm["zeros"][:, 0:P], warm["zeros"][:], start=True, stop=True)
+                nc.tensor.matmul(bank[:, :width], zeros[:, 0:P], zeros[:, :width], start=True, stop=True)
 
         def spread_biases():
             bank = new_bank()
@@ -270,17 +268,19 @@ def tile_attention_pa_kernel(
         p_es = new_operand("p_es", False)
         p_ss = [new_operand("p_ss%d" % c, False) for c in range(2)]
 
-        warm_up(5)
+        warm_up(14, 128)
         transpose_slab("w_ss0", [0, 1, 2, 3])
-        warm_up(1)
+        warm_up(1, 512)
         transpose_slab("x_ss0", [0, 1])
-        warm_up(1)
+        warm_up(1, 512)
         transpose_slab("x_ss0", [2])
-        warm_up(1)
+        warm_up(1, 512)
         bias = spread_biases()
         bias_ss = [bias[:, 4 * g2 : 4 * g2 + 4] for g2 in range(PASSES)]
         bias_es = [bias[:, 8 + 4 * g2 : 8 + 4 * g2 + 4] for g2 in range(PASSES)]
         transpose_slab("x_ss0", [3])
+        sort_unit("w_ss1", 2, "V")
+        sort_unit("w_ss1", 3, "V")
         stage1("x_ss0", "w_ss0", bias_ss[0], p_ss[0], 0, [0, 1])
         transpose_slab("w_ss1", [0, 1, 2, 3])
         sort_unit("a0", 2, "S")

@@ -22,6 +22,8 @@ M = 1024
 FLOPS = 2 * 2 * (1024 + 512) * H * H
 
 
+LOADS = ["w_ss0","x_ss0","w_ss1","a0","a1","x_ss1","w_es0","x_es","w_es1"]
+
 def unit_cols(j):
     return slice(j * P, (j + 1) * P)
 
@@ -68,7 +70,7 @@ def tile_attention_pa_kernel(
             "w_ss1": strided_units(W_ss, 1),
             "x_ss1": plain_units(attendee_stmts, 1),
         }
-        for name in ["w_ss0","x_ss0","w_ss1","a0","a1","x_ss1","w_es0","x_es","w_es1"]:
+        for name in LOADS:
             units = sources[name]
             raw[name] = load_units(name, units)
         in_words = {}
@@ -268,7 +270,7 @@ def tile_attention_pa_kernel(
         p_es = new_operand("p_es", False)
         p_ss = [new_operand("p_ss%d" % c, False) for c in range(2)]
 
-        warm_up(14, 128)
+        warm_up(20, 128)
         transpose_slab("w_ss0", [0, 1, 2, 3])
         warm_up(1, 512)
         transpose_slab("x_ss0", [0, 1])

@@ -83,6 +83,8 @@ def tile_attention_pa_kernel(
         nc.vector.memset(zeros[:, 0:P], 0.0)
         nc.vector.memset(zeros[:, P:], 0.0)
         nc.vector.memset(bias_rows[:], 0.0)
+        primer = consts.tile([P, 2], BF16, name="primer")
+        nc.scalar.copy(out=primer[:], in_=zeros[:, 0:2])
         nc.scalar.dma_start(out=bias_rows[0:2, :], in_=b_ss.rearrange("(c w) -> c w", w=PACK * P))
         nc.scalar.dma_start(out=bias_rows[2:4, :], in_=b_es.rearrange("(c w) -> c w", w=PACK * P))
 
@@ -230,7 +232,7 @@ def tile_attention_pa_kernel(
                         )
                     )
 
-        def score_bank(p, out_unit, j, c, scores, vector_banks):
+        def score_bank(p, out_unit, j, c, scores, vector_banks, by_bank):
             bank = new_bank()
             mx_group(bank[:], lambda g: unit_of(p, g, j), lambda g: slab_of(operands["a%d" % c], g))
             part = slice(c * BANK, (c + 1) * BANK)
@@ -238,19 +240,20 @@ def tile_attention_pa_kernel(
                 nc.vector.tensor_copy(out=scores[:, part], in_=bank[:])
             else:
                 nc.scalar.copy(out=scores[:, part], in_=bank[:])
-            if c == 1:
+            if by_bank:
+                nc.sync.dma_start(out=out_unit[:, part], in_=scores[:, part])
+            elif c == 1:
                 nc.sync.dma_start(out=out_unit, in_=scores[:])
 
-        def stage2(p, out_units, units, vector_banks):
+        def stage2(p, out_units, units, vector_banks, by_bank=False):
             for j in units:
                 scores = outs.tile([P, M], F32, name="scores")
                 for c in range(M // BANK):
-                    score_bank(p, out_units[j], j, c, scores, vector_banks)
+                    score_bank(p, out_units[j], j, c, scores, vector_banks, by_bank)
 
         def last_scores(p, out_unit, j):
             scores = outs.tile([P, M], F32, name="scores")
-            score_bank(p, out_unit, j, 0, scores, [])
-            nc.sync.dma_start(out=out_unit[:, :BANK], in_=scores[:, :BANK])
+            score_bank(p, out_unit, j, 0, scores, [], True)
             for half in range(2):
                 bank = new_bank()
                 cols = slice(half * BANK // 2, (half + 1) * BANK // 2)
@@ -270,13 +273,9 @@ def tile_attention_pa_kernel(
         p_es = new_operand("p_es", False)
         p_ss = [new_operand("p_ss%d" % c, False) for c in range(2)]
 
-        warm_up(20, 128)
+        warm_up(14, 128)
         transpose_slab("w_ss0", [0, 1, 2, 3])
-        warm_up(1, 512)
-        transpose_slab("x_ss0", [0, 1])
-        warm_up(1, 512)
-        transpose_slab("x_ss0", [2])
-        warm_up(1, 512)
+        transpose_slab("x_ss0", [0, 1, 2])
         bias = spread_biases()
         bias_ss = [bias[:, 4 * g2 : 4 * g2 + 4] for g2 in range(PASSES)]
         bias_es = [bias[:, 8 + 4 * g2 : 8 + 4 * g2 + 4] for g2 in range(PASSES)]
@@ -324,12 +323,14 @@ def tile_attention_pa_kernel(
         stage1("x_es", "w_es0", bias_es[0], p_es, 0, [2, 3])
         stage2(p_ss[1], out_ss[1], [1], [])
         stage1("x_es", "w_es1", bias_es[1], p_es, 1, [0, 1])
-        stage2(p_ss[1], out_ss[1], [2], [])
-        stage1("x_es", "w_es1", bias_es[1], p_es, 1, [2])
-        stage2(p_ss[1], out_ss[1], [3], [1])
-        stage1("x_es", "w_es1", bias_es[1], p_es, 1, [3])
-        stage2(p_es, out_es[0], [0], [1])
-        stage2(p_es, out_es[0], [1], [1])
         settle(0)
-        stage2(p_es, out_es[0], [2], [1])
+        stage2(p_ss[1], out_ss[1], [2], [])
+        stage2(p_ss[1], out_ss[1], [3], [])
+        stage1("x_es", "w_es1", bias_es[1], p_es, 1, [2])
+        settle(0)
+        stage2(p_es, out_es[0], [0], [])
+        stage1("x_es", "w_es1", bias_es[1], p_es, 1, [3])
+        settle(0)
+        stage2(p_es, out_es[0], [1], [1], True)
+        stage2(p_es, out_es[0], [2], [1], True)
         last_scores(p_es, out_es[0][3], 3)

from contextlib import ExitStack

import concourse.mybir as mybir
from concourse.masks import make_identity

F32 = mybir.dt.float32
BF16 = mybir.dt.bfloat16
U32 = mybir.dt.uint32
U8 = mybir.dt.uint8
FP8X4 = mybir.dt.float8_e4m3fn_x4

P = 128
H = 1024
PACK = 4
PASSES = H // (P * PACK)
UNITS = 4
SLAB = UNITS * P
BANK = 512
WORDS = H // 2
M = 1024

FLOPS = 2 * 2 * (1024 + 512) * H * H


LOADS = ["w_ss0","x_ss0","w_ss1","a0","a1","x_ss1","w_es0","x_es","w_es1"]

def unit_cols(j):
    return slice(j * P, (j + 1) * P)


def tile_attention_pa_kernel(
    tc, attendee_stmts, attendee_eres, attender, W_ss, b_ss, W_es, b_es, out_0, out_1
):
    nc = tc.nc
    with ExitStack() as ctx:
        consts = ctx.enter_context(tc.tile_pool(name="consts", bufs=1))
        raws = ctx.enter_context(tc.tile_pool(name="raws", bufs=1))
        keep = ctx.enter_context(tc.tile_pool(name="keep", bufs=1))
        stage = ctx.enter_context(tc.tile_pool(name="stage", bufs=6))
        sorts = ctx.enter_context(tc.tile_pool(name="sorts", bufs=12))
        outs = ctx.enter_context(tc.tile_pool(name="outs", bufs=8))
        psum = ctx.enter_context(tc.psum_pool(name="psum", bufs=8))
        ctx.enter_context(tc.manual_schedule())

        def load_units(name, units):
            tiles = []
            for j, unit in enumerate(units):
                raw = raws.tile([P, H], BF16, name="%s_%d" % (name, j))
                nc.sync.dma_start(out=raw[:], in_=unit)
                tiles.append(raw)
            return tiles

        def plain_units(matrix, slab):
            view = matrix.rearrange("(c j r) h -> c j r h", j=UNITS, r=P)
            return [view[slab, j] for j in range(UNITS)]

        def strided_units(weight, slab):
            view = weight.rearrange("(c r t) h -> c t r h", r=P, t=PACK)
            return [view[slab, t] for t in range(UNITS)]

        raw = {}
        sources = {
            "w_es0": strided_units(W_es, 0),
            "x_es": plain_units(attendee_eres, 0),
            "w_es1": strided_units(W_es, 1),
            "a0": plain_units(attender, 0),
            "a1": plain_units(attender, 1),
            "w_ss0": strided_units(W_ss, 0),
            "x_ss0": plain_units(attendee_stmts, 0),
            "w_ss1": strided_units(W_ss, 1),
            "x_ss1": plain_units(attendee_stmts, 1),
        }
        for name in LOADS:
            units = sources[name]
            raw[name] = load_units(name, units)
        in_words = {}

        ident = consts.tile([P, P], F32, name="ident")
        make_identity(nc, ident[:])

        bias_rows = consts.tile([P, PACK * P], BF16, name="bias_rows")
        zeros = consts.tile([P, BANK], BF16, name="zeros")
        nc.vector.memset(zeros[:, 0:P], 0.0)
        nc.vector.memset(zeros[:, P:], 0.0)
        nc.vector.memset(bias_rows[:], 0.0)
        primer = consts.tile([P, 2], BF16, name="primer")
        nc.scalar.copy(out=primer[:], in_=zeros[:, 0:2])
        nc.scalar.dma_start(out=bias_rows[0:2, :], in_=b_ss.rearrange("(c w) -> c w", w=PACK * P))
        nc.scalar.dma_start(out=bias_rows[2:4, :], in_=b_es.rearrange("(c w) -> c w", w=PACK * P))

        def new_bank():
            bank = psum.tile([P, BANK], F32, name="bank", tag="bank")
            return bank

        def warm_up(passes, width):
            bank = new_bank()
            for i in range(passes):
                nc.tensor.matmul(bank[:, :width], zeros[:, 0:P], zeros[:, :width], start=True, stop=True)

        def spread_biases():
            bank = new_bank()
            words = bias_rows[:].bitcast(F32)
            for u in range(2):
                nc.tensor.transpose(bank[:, unit_cols(u)], words[:, u::2], ident[:])
            bias_pairs = consts.tile([P, 16], BF16, name="bias_pairs")
            nc.vector.tensor_copy(
                out=bias_pairs[:].bitcast(F32).rearrange("p (s u) -> p s u", u=2),
                in_=bank[:, 0 : 2 * P].rearrange("p (u s) -> p s u", u=2)[:, 0:4, :],
            )
            bias = consts.tile([P, 16], F32, name="bias")
            nc.vector.tensor_copy(out=bias[:], in_=bias_pairs[:])
            return bias

        def sort_unit(name, j, eng):
            tile = raw[name][j]
            words = sorts.tile([P, 2, WORDS // 2], F32, name="words")
            src = tile[:].bitcast(F32).rearrange("p (n u) -> p u n", u=2)
            if eng == "V": nc.vector.tensor_copy(out=words[:], in_=src)
            elif eng == "S": nc.scalar.copy(out=words[:], in_=src)
            else: nc.gpsimd.tensor_copy(out=words[:], in_=src)
            in_words[name, j] = words

        pending = []

        def settle(left):
            while len(pending) > left:
                pending.pop(0)()

        def new_operand(name, by_unit):
            shape = [P, UNITS, PASSES, P] if by_unit else [P, PASSES, SLAB]
            codes = keep.tile(shape, U32, name="%s_codes" % name, align_bytes=64)
            scales = keep.tile(shape, U8, name="%s_scales" % name, align_bytes=64)
            return codes, scales, by_unit

        def unit_of(operand, g, j):
            codes, scales, by_unit = operand
            if by_unit:
                return codes[:, j, g, :], scales[:, j, g, :]
            return codes[:, g, unit_cols(j)], scales[:, g, unit_cols(j)]

        def slab_of(operand, g):
            codes, scales, by_unit = operand
            return codes[:, g, :], scales[:, g, :]

        def quantise(grouped, target):
            codes, scales = target
            nc.vector.quantize_mx(out=codes.bitcast(FP8X4), scales=scales, in_=grouped)

        def transpose_unit(key, grouped, half, ev):
            tile = raw[key[0]][key[1]]
            bank = new_bank()
            words = in_words.get(key)
            for g in range(PASSES):
                for u in range(2):
                    if words is None:
                        first_word = g * 2 * P + u
                        source = tile[:].bitcast(F32)[:, first_word : first_word + 2 * P - 1 : 2]
                    else:
                        source = words[:, u, unit_cols(g)]
                    nc.tensor.transpose(bank[:, unit_cols(2 * g + u)], source, ident[:])
            (nc.vector.tensor_copy if str(key[1]) in ev else nc.scalar.copy)(
                out=grouped[:].bitcast(F32).rearrange("p (g h r u) -> p g h r u", g=PASSES, r=P, u=2)[:, :, half],
                in_=bank[:].rearrange("p (g u r) -> p g r u", g=PASSES, u=2),
            )

        def transpose_slab(name, units, ev=""):
            operand = operands.get(name) or new_operand(name, name[0] != "a")
            operands[name] = operand
            codes, scales, by_unit = operand
            step = 1 if by_unit else 2
            for j in units[::step]:
                grouped = stage.tile([P, step * H], BF16, name="grouped%d" % step, align_bytes=64)
                for half in range(step):
                    transpose_unit((name, j + half), grouped, half, ev)
                    if half + 1 < step:
                        settle(0)

                def finish(grouped=grouped, j=j):
                    if by_unit:
                        targets = [[part[:, j].rearrange("p g r -> p (g r)") for part in (codes, scales)]]
                    else:
                        cols = slice(j * P, (j + 2) * P)
                        targets = [[part[:, g, cols] for part in (codes, scales)] for g in range(PASSES)]
                    for i, target in enumerate(targets):
                        width = step * H // len(targets)
                        quantise(grouped[:, i * width : (i + 1) * width], target)

                pending.append(finish)
                settle(1)

        def mx_group(out, stationary, moving):
            for g in range(PASSES):
                lhs, rhs = stationary(g), moving(g)
                nc.tensor.matmul_mx(
                    out=out,
                    lhsT=lhs[0].bitcast(FP8X4),
                    lhsT_scale=lhs[1],
                    rhs=rhs[0].bitcast(FP8X4),
                    rhs_scale=rhs[1],
                    start=(g == 0),
                    stop=(g == PASSES - 1),
                )

        def stage1(x, w, bias_cols, p, g2, units):
            x, w = operands[x], operands[w]
            group = []
            for j in units:
                bank = new_bank()
                for t in range(PACK):
                    mx_group(
                        bank[:, unit_cols(t)],
                        lambda g, t=t: unit_of(w, g, t),
                        lambda g, j=j: unit_of(x, g, j),
                    )
                if len(group) == 0:
                    p_grouped = stage.tile([P, 2 * P, PACK], BF16, name="p_grouped", align_bytes=64)
                nc.vector.tensor_tensor(
                    out=p_grouped[:, len(group) * P : (len(group) + 1) * P, :],
                    in0=bank[:].rearrange("p (t s) -> p s t", t=PACK),
                    in1=bias_cols.unsqueeze(1).to_broadcast([P, P, PACK]),
                    op=mybir.AluOpType.add,
                )
                group.append(j)
                settle(0)
                if len(group) == 2 or j == units[-1]:
                    cols = slice(group[0] * P, (group[-1] + 1) * P)
                    used = len(group) * P
                    group = []
                    pending.append(
                        lambda tile=p_grouped, cols=cols, used=used: quantise(
                            tile[:, :used, :].rearrange("p s t -> p (s t)"), [part[:, g2, cols] for part in p[:2]]
                        )
                    )

        def score_bank(p, out_unit, j, c, scores, vector_banks, by_bank):
            bank = new_bank()
            mx_group(bank[:], lambda g: unit_of(p, g, j), lambda g: slab_of(operands["a%d" % c], g))
            part = slice(c * BANK, (c + 1) * BANK)
            if c in vector_banks:
                nc.vector.tensor_copy(out=scores[:, part], in_=bank[:])
            else:
                nc.scalar.copy(out=scores[:, part], in_=bank[:])
            if by_bank:
                nc.sync.dma_start(out=out_unit[:, part], in_=scores[:, part])
            elif c == 1:
                nc.sync.dma_start(out=out_unit, in_=scores[:])

        def stage2(p, out_units, units, vector_banks, by_bank=False):
            for j in units:
                scores = outs.tile([P, M], F32, name="scores")
                for c in range(M // BANK):
                    score_bank(p, out_units[j], j, c, scores, vector_banks, by_bank)

        def last_scores(p, out_unit, j):
            scores = outs.tile([P, M], F32, name="scores")
            score_bank(p, out_unit, j, 0, scores, [], True)
            for half in range(2):
                bank = new_bank()
                cols = slice(half * BANK // 2, (half + 1) * BANK // 2)
                mx_group(
                    bank[:, : BANK // 2],
                    lambda g: unit_of(p, g, j),
                    lambda g: tuple(part[:, cols] for part in slab_of(operands["a1"], g)),
                )
                part = slice(BANK + half * BANK // 2, BANK + (half + 1) * BANK // 2)
                copy = nc.scalar.copy if half else nc.vector.tensor_copy
                copy(out=scores[:, part], in_=bank[:, : BANK // 2])
                nc.sync.dma_start(out=out_unit[:, part], in_=scores[:, part])

        out_es = out_1.rearrange("(c j r) m -> c j r m", j=UNITS, r=P)
        out_ss = out_0.rearrange("(c j r) m -> c j r m", j=UNITS, r=P)
        operands = {}
        p_es = new_operand("p_es", False)
        p_ss = [new_operand("p_ss%d" % c, False) for c in range(2)]

        warm_up(14, 128)
        transpose_slab("w_ss0", [0, 1, 2, 3])
        transpose_slab("x_ss0", [0, 1, 2])
        bias = spread_biases()
        bias_ss = [bias[:, 4 * g2 : 4 * g2 + 4] for g2 in range(PASSES)]
        bias_es = [bias[:, 8 + 4 * g2 : 8 + 4 * g2 + 4] for g2 in range(PASSES)]
        transpose_slab("x_ss0", [3])
        sort_unit("w_ss1", 2, "V")
        sort_unit("w_ss1", 3, "V")
        stage1("x_ss0", "w_ss0", bias_ss[0], p_ss[0], 0, [0, 1])
        transpose_slab("w_ss1", [0, 1, 2, 3])
        sort_unit("a0", 2, "S")
        sort_unit("a0", 3, "V")
        stage1("x_ss0", "w_ss0", bias_ss[0], p_ss[0], 0, [2, 3])
        transpose_slab("a0", [0, 1, 2, 3])
        sort_unit("a1", 2, "S")
        sort_unit("a1", 3, "V")
        stage1("x_ss0", "w_ss1", bias_ss[1], p_ss[0], 1, [0, 1])
        transpose_slab("a1", [0, 1, 2, 3])
        sort_unit("x_ss1", 2, "S")
        sort_unit("x_ss1", 3, "V")
        stage1("x_ss0", "w_ss1", bias_ss[1], p_ss[0], 1, [2, 3])
        sort_unit("w_es0", 0, "V")
        sort_unit("w_es0", 1, "V")
        sort_unit("w_es0", 2, "V")
        sort_unit("w_es0", 3, "V")
        transpose_slab("x_ss1", [0, 1, 2, 3])
        settle(0)
        stage2(p_ss[0], out_ss[0], [0, 1], [])
        sort_unit("x_es", 0, "V")
        sort_unit("x_es", 1, "V")
        sort_unit("x_es", 2, "V")
        sort_unit("x_es", 3, "V")
        transpose_slab("w_es0", [0, 1, 2, 3])
        stage2(p_ss[0], out_ss[0], [2, 3], [])
        stage1("x_ss1", "w_ss0", bias_ss[0], p_ss[1], 0, [0, 1])
        sort_unit("w_es1", 0, "V")
        sort_unit("w_es1", 1, "V")
        sort_unit("w_es1", 2, "V")
        sort_unit("w_es1", 3, "V")
        transpose_slab("x_es", [0, 1, 2, 3])
        stage1("x_ss1", "w_ss0", bias_ss[0], p_ss[1], 0, [2, 3])
        stage1("x_ss1", "w_ss1", bias_ss[1], p_ss[1], 1, [0, 1])
        transpose_slab("w_es1", [0, 1, 2, 3])
        stage1("x_ss1", "w_ss1", bias_ss[1], p_ss[1], 1, [2, 3])
        stage1("x_es", "w_es0", bias_es[0], p_es, 0, [0, 1])
        stage2(p_ss[1], out_ss[1], [0], [])
        stage1("x_es", "w_es0", bias_es[0], p_es, 0, [2, 3])
        stage2(p_ss[1], out_ss[1], [1], [])
        stage1("x_es", "w_es1", bias_es[1], p_es, 1, [0, 1])
        settle(0)
        stage2(p_ss[1], out_ss[1], [2], [])
        stage2(p_ss[1], out_ss[1], [3], [])
        stage1("x_es", "w_es1", bias_es[1], p_es, 1, [2])
        settle(0)
        stage2(p_es, out_es[0], [0], [])
        stage1("x_es", "w_es1", bias_es[1], p_es, 1, [3])
        settle(0)
        stage2(p_es, out_es[0], [1], [1], True)
        stage2(p_es, out_es[0], [2], [1], True)
        last_scores(p_es, out_es[0][3], 3)
